import numpy as np
import ml_dtypes


def mxq(x, axis, fmt="e4m3"):
    dtype, down = {"e4m3": (ml_dtypes.float8_e4m3fn, 7), "e5m2": (ml_dtypes.float8_e5m2, 14)}[fmt]
    v = np.moveaxis(np.asarray(x, np.float32).astype(ml_dtypes.bfloat16).astype(np.float64), axis, -1)
    blocks = v.reshape(v.shape[:-1] + (-1, 32))
    amax = np.abs(blocks).max(-1, keepdims=True)
    byte = np.maximum(np.where(amax > 0, np.frexp(amax)[1] - 1 + 127, 0) - down, 1)
    scale = np.exp2(byte - 127.0)
    codes = (blocks / scale).astype(np.float32).astype(dtype).astype(np.float64)
    return np.moveaxis((codes * scale).reshape(v.shape), -1, axis)


WIDE = False


def mx_kscale(k):
    if not WIDE:
        return np.ones(k)
    levels = np.array([10, -10, 5, -5, 0])
    a = np.random.permutation(np.resize(levels, k // 512 * 4)).reshape(k // 512, 4)
    idx = np.arange(k)
    return np.exp2(a[idx // 512, idx % 128 // 32])


BF16 = ml_dtypes.bfloat16


def bf(x):
    return np.asarray(x, np.float32).astype(BF16)


def f64(x):
    return np.asarray(x).astype(np.float64)


S, HID, H, KV, D, WINDOW, QB = 4096, 1024, 4, 2, 128, 512, 512
NQ, NK = H * D, KV * D
EPS = 1e-6
ROPE_THETA = 10000.0


def rms_norm(x, w):
    var = np.mean(x * x, axis=-1, keepdims=True)
    return x * (1.0 / np.sqrt(var + EPS)) * (1.0 + w)


def rotate_half(x):
    x1, x2 = np.split(x, 2, axis=-1)
    return np.concatenate([-x2, x1], axis=-1)


def apply_rope(x, cos, sin):
    return x * cos[:, None, :] + rotate_half(x) * sin[:, None, :]


def setup_inputs():
    s = mx_kscale(HID)
    inv_freq = 1.0 / ROPE_THETA ** (np.arange(0, D, 2) / D)
    freqs = np.outer(np.arange(S), inv_freq)
    emb = np.concatenate([freqs, freqs], -1)
    return {"hidden_states": bf(np.random.standard_normal((S, HID)) * s),
            "w_qkv": bf(np.random.standard_normal((HID, NQ + NK + NK)) / np.sqrt(HID) / s[:, None]),
            "q_norm_w": bf(1.0 + 0.1 * np.random.standard_normal(D)),
            "k_norm_w": bf(1.0 + 0.1 * np.random.standard_normal(D)),
            "cos": bf(np.cos(emb)), "sin": bf(np.sin(emb))}


def reference(hidden_states, w_qkv, q_norm_w, k_norm_w, cos, sin):
    qkv = mxq(f64(hidden_states), 1, "e4m3") @ mxq(f64(w_qkv), 0, "e4m3")
    q = qkv[:, :NQ].reshape(S, H, D)
    k = qkv[:, NQ:NQ + NK].reshape(S, KV, D)
    v = qkv[:, NQ + NK:].reshape(S, KV, D)
    q = rms_norm(q, f64(q_norm_w))
    k = rms_norm(k, f64(k_norm_w))
    q = apply_rope(q, f64(cos), f64(sin))
    k = apply_rope(k, f64(cos), f64(sin))
    return q, k, v

@@ -1,0 +1,210 @@
+from contextlib import ExitStack
+
+import concourse.mybir as mybir
+from concourse.masks import make_identity
+
+F32 = mybir.dt.float32
+BF16 = mybir.dt.bfloat16
+U32 = mybir.dt.uint32
+U8 = mybir.dt.uint8
+FP8X4 = mybir.dt.float8_e4m3fn_x4
+ALU = mybir.AluOpType
+ACT = mybir.ActivationFunctionType
+
+P = 128
+SEQ = 4096
+HID = 1024
+D = 128
+HALF = D // 2
+Q_HEADS = 4
+K_HEADS = 2
+ROPE_HEADS = Q_HEADS + K_HEADS
+N_OUT = 1024
+BANK = 512
+EPS = 1e-6
+
+K_PASS = 512
+PASSES = HID // K_PASS
+WORDS = HID // 2
+TILES = SEQ // P
+GROUP = 4
+GROUPS = TILES // GROUP
+STORE = 2
+
+FLOPS = 2 * SEQ * HID * N_OUT
+
+
+def tile_gemmaattention_pa_t_kernel(
+    tc, hidden_states, w_qkv, q_norm_w, k_norm_w, cos, sin, out_0, out_1, out_2
+):
+    nc = tc.nc
+
+    hid_rows = hidden_states.rearrange("(p t) k -> p t k", t=TILES)
+    cos_rows = cos.rearrange("(p t) d -> p t d", t=TILES)
+    sin_rows = sin.rearrange("(p t) d -> p t d", t=TILES)
+    q_rows = out_0.rearrange("(p t) h d -> p t (h d)", t=TILES)
+    k_rows = out_1.rearrange("(p t) h d -> p t (h d)", t=TILES)
+    v_rows = out_2.rearrange("(p t) h d -> p t (h d)", t=TILES)
+    w_rows = w_qkv.rearrange("(c u p e) n -> p c u (e n)", c=PASSES, u=2, p=P, e=2)
+
+    with ExitStack() as ctx:
+        keep = ctx.enter_context(tc.tile_pool(name="keep", bufs=1))
+        prep = ctx.enter_context(tc.tile_pool(name="prep", bufs=2))
+        work = ctx.enter_context(tc.tile_pool(name="work", bufs=3))
+        psum_keep = ctx.enter_context(tc.psum_pool(name="psum_keep", bufs=1))
+        psum_turn = ctx.enter_context(tc.psum_pool(name="psum_turn", bufs=2))
+        psum_acc = ctx.enter_context(tc.psum_pool(name="psum_acc", bufs=2))
+
+        hid_sb = keep.tile([P, TILES, HID], BF16)
+        w_raw = keep.tile([P, PASSES, 2, 2 * N_OUT], BF16)
+        cos_sb = keep.tile([P, TILES, D], BF16)
+        sin_sb = keep.tile([P, TILES, D], BF16)
+        nc.sync.dma_start(out=hid_sb[:, 0:GROUP, :], in_=hid_rows[:, 0:GROUP, :])
+        for c in range(PASSES):
+            nc.sync.dma_start(out=w_raw[:, c], in_=w_rows[:, c])
+        nc.sync.dma_start(out=cos_sb[:], in_=cos_rows)
+        nc.sync.dma_start(out=sin_sb[:], in_=sin_rows)
+        for g in range(1, GROUPS):
+            tiles = slice(g * GROUP, (g + 1) * GROUP)
+            nc.sync.dma_start(out=hid_sb[:, tiles, :], in_=hid_rows[:, tiles, :])
+
+        ident = keep.tile([P, P], F32)
+        make_identity(nc, ident[:])
+
+        gain_rows = keep.tile([P, 2 * D], BF16)
+        nc.vector.memset(gain_rows[:], 0.0)
+        nc.vector.memset(gain_rows[32:33, :], 1.0)
+        nc.scalar.dma_start(out=gain_rows[0:1, 0:D], in_=q_norm_w.rearrange("(o d) -> o d", o=1))
+        nc.scalar.dma_start(out=gain_rows[0:1, D : 2 * D], in_=k_norm_w.rearrange("(o d) -> o d", o=1))
+        ones = keep.tile([P, P], BF16)
+        nc.vector.memset(ones[:], 1.0)
+        gain_ps = psum_keep.tile([P, 2, D], F32)
+        nc.tensor.matmul(
+            gain_ps[:].rearrange("p c d -> p (c d)"), lhsT=ones[:], rhs=gain_rows[:], start=True, stop=True
+        )
+
+        w_grouped = keep.tile([P, PASSES, N_OUT, 4], BF16, align_bytes=64)
+        w_codes = keep.tile([P, PASSES, N_OUT], U32, align_bytes=64)
+        w_scales = keep.tile([P, PASSES, N_OUT], U8, align_bytes=64)
+        for c in range(PASSES):
+            four_rows = w_raw[:, c].rearrange("p u (e n) -> p (u e) n", e=2)
+            nc.vector.tensor_copy(
+                out=w_grouped[:, c].rearrange("p (a i) t -> p a t i", i=4),
+                in_=four_rows.rearrange("p t (a i) -> p a t i", i=4),
+            )
+        for c in range(PASSES):
+            nc.vector.quantize_mx(
+                out=w_codes[:, c, :].bitcast(FP8X4),
+                scales=w_scales[:, c, :],
+                in_=w_grouped[:, c].rearrange("p n t -> p (n t)"),
+            )
+
+        hid_words = hid_sb[:].bitcast(F32)
+
+        def prepare(g):
+            first = g * GROUP
+            hid_grouped = prep.tile([P, GROUP, HID], BF16, align_bytes=64)
+            grouped_words = hid_grouped[:].bitcast(F32)
+            for i in range(GROUP):
+                turned = psum_turn.tile([P, 2 * PASSES, P], F32)
+                for b in range(2 * PASSES):
+                    nc.tensor.transpose(
+                        turned[:, b, :], hid_words[:, first + i, b * P : (b + 1) * P], ident[:]
+                    )
+                nc.scalar.copy(
+                    out=grouped_words[:, i, :].rearrange("p (c s u) -> p c s u", c=PASSES, u=2),
+                    in_=turned[:].rearrange("p (c u) s -> p c s u", u=2),
+                )
+            hid_codes = prep.tile([P, GROUP * PASSES * P], U32, align_bytes=64)
+            hid_scales = prep.tile([P, GROUP * PASSES * P], U8, align_bytes=64)
+            nc.vector.quantize_mx(
+                out=hid_codes[:].bitcast(FP8X4),
+                scales=hid_scales[:],
+                in_=hid_grouped[:].rearrange("p g k -> p (g k)"),
+            )
+
+            table = prep.tile([P, GROUP, 2, 2, D], F32)
+            tiles = slice(first, first + GROUP)
+            gain_all = gain_ps[:].unsqueeze(1)
+            nc.vector.tensor_tensor(
+                out=table[:, :, :, 0, :],
+                in0=gain_all.to_broadcast([P, GROUP, 2, D]),
+                in1=cos_sb[:, tiles, :].unsqueeze(2).to_broadcast([P, GROUP, 2, D]),
+                op=ALU.mult,
+            )
+            for here, there in ((slice(0, HALF), slice(HALF, D)), (slice(HALF, D), slice(0, HALF))):
+                nc.vector.tensor_tensor(
+                    out=table[:, :, :, 1, here],
+                    in0=gain_all[:, :, :, here].to_broadcast([P, GROUP, 2, HALF]),
+                    in1=sin_sb[:, tiles, there].unsqueeze(2).to_broadcast([P, GROUP, 2, HALF]),
+                    op=ALU.mult,
+                )
+            return hid_codes, hid_scales, table
+
+        def project_norm_rotate(i, hid_codes, hid_scales, table, result):
+            q_ps = psum_acc.tile([P, BANK], F32)
+            kv_ps = psum_acc.tile([P, BANK], F32)
+            for c in range(PASSES):
+                rows = slice((i * PASSES + c) * P, (i * PASSES + c + 1) * P)
+                for bank, cols in ((q_ps, slice(0, BANK)), (kv_ps, slice(BANK, 2 * BANK))):
+                    nc.tensor.matmul_mx(
+                        out=bank[:],
+                        lhsT=hid_codes[:, rows].bitcast(FP8X4),
+                        lhsT_scale=hid_scales[:, rows],
+                        rhs=w_codes[:, c, cols].bitcast(FP8X4),
+                        rhs_scale=w_scales[:, c, cols],
+                        start=(c == 0),
+                        stop=(c == PASSES - 1),
+                    )
+            heads = [q_ps[:, h * D : (h + 1) * D] for h in range(Q_HEADS)]
+            heads += [kv_ps[:, h * D : (h + 1) * D] for h in range(K_HEADS)]
+
+            squares = work.tile([P, ROPE_HEADS, D], BF16)
+            sum_sq = work.tile([P, ROPE_HEADS], F32)
+            for h in range(ROPE_HEADS):
+                nc.scalar.activation(
+                    out=squares[:, h, :], in_=heads[h], func=ACT.Square, accum_out=sum_sq[:, h : h + 1]
+                )
+            nc.scalar.copy(out=result[:, ROPE_HEADS * D : N_OUT], in_=kv_ps[:, K_HEADS * D : BANK])
+            inv_rms = work.tile([P, ROPE_HEADS], F32)
+            nc.scalar.activation(
+                out=inv_rms[:], in_=sum_sq[:], func=ACT.Abs_reciprocal_sqrt, scale=1.0 / D, bias=EPS
+            )
+
+            products = work.tile([P, ROPE_HEADS, 2, D], F32)
+            for h in range(ROPE_HEADS):
+                nc.vector.scalar_tensor_tensor(
+                    out=products[:, h],
+                    in0=heads[h].unsqueeze(1).to_broadcast([P, 2, D]),
+                    scalar=inv_rms[:, h : h + 1],
+                    in1=table[:, i, 0 if h < Q_HEADS else 1],
+                    op0=ALU.mult,
+                    op1=ALU.mult,
+                )
+            rotated = result[:, 0 : ROPE_HEADS * D].rearrange("p (h d) -> p h d", d=D)
+            nc.gpsimd.tensor_tensor(
+                out=rotated[:, :, 0:HALF],
+                in0=products[:, :, 0, 0:HALF],
+                in1=products[:, :, 1, HALF:D],
+                op=ALU.subtract,
+            )
+            nc.gpsimd.tensor_tensor(
+                out=rotated[:, :, HALF:D],
+                in0=products[:, :, 0, HALF:D],
+                in1=products[:, :, 1, 0:HALF],
+                op=ALU.add,
+            )
+
+        ready = prepare(0)
+        for g in range(GROUPS):
+            current = ready
+            if g + 1 < GROUPS:
+                ready = prepare(g + 1)
+            for half in range(GROUP // STORE):
+                results = work.tile([P, STORE, N_OUT], F32)
+                for j in range(STORE):
+                    project_norm_rotate(half * STORE + j, current[0], current[1], current[2], results[:, j, :])
+                tiles = slice(g * GROUP + half * STORE, g * GROUP + (half + 1) * STORE)
+                nc.sync.dma_start(out=q_rows[:, tiles, :], in_=results[:, :, 0 : Q_HEADS * D])
+                nc.sync.dma_start(out=k_rows[:, tiles, :], in_=results[:, :, Q_HEADS * D : ROPE_HEADS * D])
+                nc.sync.dma_start(out=v_rows[:, tiles, :], in_=results[:, :, ROPE_HEADS * D : N_OUT])

@@ -19,17 +19,27 @@ HALF = D // 2
 Q_HEADS = 4
 K_HEADS = 2
 ROPE_HEADS = Q_HEADS + K_HEADS
+ROPE_COLS = ROPE_HEADS * D
 N_OUT = 1024
 BANK = 512
 EPS = 1e-6
 
 K_PASS = 512
 PASSES = HID // K_PASS
-WORDS = HID // 2
+WORD_BLOCKS = HID // 2 // P
 TILES = SEQ // P
-GROUP = 4
-GROUPS = TILES // GROUP
-STORE = 2
+PAIR = 2
+
+LEAD_TURN = 5
+LEAD_GROUP = 4
+LEAD_QUANTISE = 3
+LEAD_PROJECT = 2
+LEAD_NORM = 1
+LAG_ADD = 1
+LAG_STORE = 2
+LEAD_TABLE = 7
+HEAD_TABLES = 4
+EARLY_ANGLES = 8
 
 FLOPS = 2 * SEQ * HID * N_OUT
 
@@ -48,49 +58,193 @@ def tile_gemmaattention_pa_t_kernel(
     w_rows = w_qkv.rearrange("(c u p e) n -> p c u (e n)", c=PASSES, u=2, p=P, e=2)
 
     with ExitStack() as ctx:
+        ctx.enter_context(tc.manual_schedule())
         keep = ctx.enter_context(tc.tile_pool(name="keep", bufs=1))
-        prep = ctx.enter_context(tc.tile_pool(name="prep", bufs=2))
-        work = ctx.enter_context(tc.tile_pool(name="work", bufs=3))
-        psum_keep = ctx.enter_context(tc.psum_pool(name="psum_keep", bufs=1))
+        stage = ctx.enter_context(tc.tile_pool(name="stage", bufs=3))
+        tables = ctx.enter_context(tc.tile_pool(name="tables", bufs=LEAD_TABLE + 1))
+        leave = ctx.enter_context(tc.tile_pool(name="leave", bufs=4))
+        psum_gain = ctx.enter_context(tc.psum_pool(name="psum_gain", bufs=1))
         psum_turn = ctx.enter_context(tc.psum_pool(name="psum_turn", bufs=2))
-        psum_acc = ctx.enter_context(tc.psum_pool(name="psum_acc", bufs=2))
+        psum_q = ctx.enter_context(tc.psum_pool(name="psum_q", bufs=3))
+        psum_kv = ctx.enter_context(tc.psum_pool(name="psum_kv", bufs=2))
 
         hid_sb = keep.tile([P, TILES, HID], BF16)
         w_raw = keep.tile([P, PASSES, 2, 2 * N_OUT], BF16)
         cos_sb = keep.tile([P, TILES, D], BF16)
         sin_sb = keep.tile([P, TILES, D], BF16)
-        nc.sync.dma_start(out=hid_sb[:, 0:GROUP, :], in_=hid_rows[:, 0:GROUP, :])
+        gain_rows = keep.tile([P, 2 * D], BF16)
+        nc.vector.memset(gain_rows[:], 0.0)
+        nc.vector.memset(gain_rows[32:33, :], 1.0)
+        nc.sync.dma_start(out=gain_rows[0:1, 0:D], in_=q_norm_w.rearrange("(o d) -> o d", o=1))
+        nc.sync.dma_start(out=gain_rows[0:1, D : 2 * D], in_=k_norm_w.rearrange("(o d) -> o d", o=1))
+
+        def load_hidden(first, last):
+            for t in range(first, last, PAIR):
+                nc.sync.dma_start(out=hid_sb[:, t : t + PAIR, :], in_=hid_rows[:, t : t + PAIR, :])
+
+        nc.sync.dma_start(out=cos_sb[:, 0:EARLY_ANGLES, :], in_=cos_rows[:, 0:EARLY_ANGLES, :])
+        nc.sync.dma_start(out=sin_sb[:, 0:EARLY_ANGLES, :], in_=sin_rows[:, 0:EARLY_ANGLES, :])
         for c in range(PASSES):
             nc.sync.dma_start(out=w_raw[:, c], in_=w_rows[:, c])
-        nc.sync.dma_start(out=cos_sb[:], in_=cos_rows)
-        nc.sync.dma_start(out=sin_sb[:], in_=sin_rows)
-        for g in range(1, GROUPS):
-            tiles = slice(g * GROUP, (g + 1) * GROUP)
-            nc.sync.dma_start(out=hid_sb[:, tiles, :], in_=hid_rows[:, tiles, :])
+        load_hidden(0, EARLY_ANGLES)
+        nc.sync.dma_start(out=cos_sb[:, EARLY_ANGLES:TILES, :], in_=cos_rows[:, EARLY_ANGLES:TILES, :])
+        nc.sync.dma_start(out=sin_sb[:, EARLY_ANGLES:TILES, :], in_=sin_rows[:, EARLY_ANGLES:TILES, :])
+        load_hidden(EARLY_ANGLES, TILES)
+
+        warm = keep.tile([P, 1], F32)
+        nc.vector.memset(warm[:], 1.0)
+        nc.scalar.activation(out=warm[:], in_=warm[:], func=ACT.Abs_reciprocal_sqrt)
 
         ident = keep.tile([P, P], F32)
         make_identity(nc, ident[:])
 
-        gain_rows = keep.tile([P, 2 * D], BF16)
-        nc.vector.memset(gain_rows[:], 0.0)
-        nc.vector.memset(gain_rows[32:33, :], 1.0)
-        nc.scalar.dma_start(out=gain_rows[0:1, 0:D], in_=q_norm_w.rearrange("(o d) -> o d", o=1))
-        nc.scalar.dma_start(out=gain_rows[0:1, D : 2 * D], in_=k_norm_w.rearrange("(o d) -> o d", o=1))
         ones = keep.tile([P, P], BF16)
         nc.vector.memset(ones[:], 1.0)
-        gain_ps = psum_keep.tile([P, 2, D], F32)
+        gain_ps = psum_gain.tile([P, 2, D], F32)
         nc.tensor.matmul(
             gain_ps[:].rearrange("p c d -> p (c d)"), lhsT=ones[:], rhs=gain_rows[:], start=True, stop=True
         )
 
+        hid_words = hid_sb[:].bitcast(F32)
         w_grouped = keep.tile([P, PASSES, N_OUT, 4], BF16, align_bytes=64)
         w_codes = keep.tile([P, PASSES, N_OUT], U32, align_bytes=64)
         w_scales = keep.tile([P, PASSES, N_OUT], U8, align_bytes=64)
+
+        table = {}
+        turned = {}
+        grouped = {}
+        hid_codes = {}
+        hid_scales = {}
+        q_ps = {}
+        kv_ps = {}
+        inv_rms = {}
+        products = {}
+        results = {}
+
+        def make_table(i):
+            table[i] = tables.tile([P, 2, 2, D], F32, name="table")
+            nc.vector.tensor_tensor(
+                out=table[i][:, :, 0, :],
+                in0=gain_ps[:],
+                in1=cos_sb[:, i, :].unsqueeze(1).to_broadcast([P, 2, D]),
+                op=ALU.mult,
+            )
+            for here, there in ((slice(0, HALF), slice(HALF, D)), (slice(HALF, D), slice(0, HALF))):
+                nc.vector.tensor_tensor(
+                    out=table[i][:, :, 1, here],
+                    in0=gain_ps[:, :, here],
+                    in1=sin_sb[:, i, there].unsqueeze(1).to_broadcast([P, 2, HALF]),
+                    op=ALU.mult,
+                )
+
+        def turn_hidden(i):
+            turned[i] = psum_turn.tile([P, WORD_BLOCKS, P], F32, name="turned")
+            for b in range(WORD_BLOCKS):
+                nc.tensor.transpose(turned[i][:, b, :], hid_words[:, i, b * P : (b + 1) * P], ident[:])
+
+        def group_hidden(i):
+            grouped[i] = stage.tile([P, HID], BF16, name="grouped", align_bytes=64)
+            nc.scalar.copy(
+                out=grouped[i][:].bitcast(F32).rearrange("p (c s u) -> p c s u", c=PASSES, u=2),
+                in_=turned[i][:].rearrange("p (c u) s -> p c s u", u=2),
+            )
+
+        def quantise_hidden(i):
+            hid_codes[i] = stage.tile([P, PASSES * P], U32, name="hid_codes", align_bytes=64)
+            hid_scales[i] = stage.tile([P, PASSES * P], U8, name="hid_scales", align_bytes=64)
+            nc.vector.quantize_mx(
+                out=hid_codes[i][:].bitcast(FP8X4), scales=hid_scales[i][:], in_=grouped[i][:]
+            )
+
+        def project(i):
+            q_ps[i] = psum_q.tile([P, BANK], F32, name="q_ps")
+            kv_ps[i] = psum_kv.tile([P, BANK], F32, name="kv_ps")
+            for bank, cols in ((q_ps[i], slice(0, BANK)), (kv_ps[i], slice(BANK, 2 * BANK))):
+                for c in range(PASSES):
+                    rows = slice(c * P, (c + 1) * P)
+                    nc.tensor.matmul_mx(
+                        out=bank[:],
+                        lhsT=hid_codes[i][:, rows].bitcast(FP8X4),
+                        lhsT_scale=hid_scales[i][:, rows],
+                        rhs=w_codes[:, c, cols].bitcast(FP8X4),
+                        rhs_scale=w_scales[:, c, cols],
+                        start=(c == 0),
+                        stop=(c == PASSES - 1),
+                    )
+
+        def head_of(i, h):
+            if h < Q_HEADS:
+                return q_ps[i][:, h * D : (h + 1) * D]
+            return kv_ps[i][:, (h - Q_HEADS) * D : (h - Q_HEADS + 1) * D]
+
+        def result_of(i):
+            return results[i // PAIR][:, i % PAIR, :]
+
+        def norm(i):
+            if i % PAIR == 0:
+                results[i // PAIR] = leave.tile([P, PAIR, N_OUT], F32, name="results")
+            squares = stage.tile([P, ROPE_HEADS, D], BF16, name="squares")
+            sum_sq = stage.tile([P, ROPE_HEADS], F32, name="sum_sq")
+            for h in range(ROPE_HEADS):
+                nc.scalar.activation(
+                    out=squares[:, h, :], in_=head_of(i, h), func=ACT.Square, accum_out=sum_sq[:, h : h + 1]
+                )
+            nc.scalar.copy(out=result_of(i)[:, ROPE_COLS:N_OUT], in_=kv_ps[i][:, K_HEADS * D : BANK])
+            inv_rms[i] = stage.tile([P, ROPE_HEADS], F32, name="inv_rms")
+            nc.scalar.activation(
+                out=inv_rms[i][:], in_=sum_sq[:], func=ACT.Abs_reciprocal_sqrt, scale=1.0 / D, bias=EPS
+            )
+
+        def multiply(i):
+            products[i] = stage.tile([P, ROPE_HEADS, 2, D], F32, name="products")
+            for h in list(range(Q_HEADS, ROPE_HEADS)) + list(range(Q_HEADS)):
+                nc.vector.scalar_tensor_tensor(
+                    out=products[i][:, h],
+                    in0=head_of(i, h).unsqueeze(1).to_broadcast([P, 2, D]),
+                    scalar=inv_rms[i][:, h : h + 1],
+                    in1=table[i][:, 0 if h < Q_HEADS else 1],
+                    op0=ALU.mult,
+                    op1=ALU.mult,
+                )
+
+        def add_halves(i):
+            rotated = result_of(i)[:, 0:ROPE_COLS].rearrange("p (h d) -> p h d", d=D)
+            nc.gpsimd.tensor_tensor(
+                out=rotated[:, :, 0:HALF],
+                in0=products[i][:, :, 0, 0:HALF],
+                in1=products[i][:, :, 1, HALF:D],
+                op=ALU.subtract,
+            )
+            nc.gpsimd.tensor_tensor(
+                out=rotated[:, :, HALF:D],
+                in0=products[i][:, :, 0, HALF:D],
+                in1=products[i][:, :, 1, 0:HALF],
+                op=ALU.add,
+            )
+
+        def store(i):
+            if i % PAIR != PAIR - 1:
+                return
+            pair = results[i // PAIR]
+            tiles = slice(i - PAIR + 1, i + 1)
+            nc.sync.dma_start(out=q_rows[:, tiles, :], in_=pair[:, :, 0 : Q_HEADS * D])
+            nc.sync.dma_start(out=k_rows[:, tiles, :], in_=pair[:, :, Q_HEADS * D : ROPE_COLS])
+            nc.sync.dma_start(out=v_rows[:, tiles, :], in_=pair[:, :, ROPE_COLS:N_OUT])
+
+        for i in range(HEAD_TABLES):
+            make_table(i)
+
+        rope_cols = slice(0, ROPE_COLS)
+        v_cols = slice(ROPE_COLS, N_OUT)
         for c in range(PASSES):
             four_rows = w_raw[:, c].rearrange("p u (e n) -> p (u e) n", e=2)
             nc.vector.tensor_copy(
-                out=w_grouped[:, c].rearrange("p (a i) t -> p a t i", i=4),
-                in_=four_rows.rearrange("p t (a i) -> p a t i", i=4),
+                out=w_grouped[:, c, rope_cols, :].rearrange("p (a i) t -> p a t i", i=4),
+                in_=four_rows[:, :, rope_cols].rearrange("p t (a i) -> p a t i", i=4),
+            )
+            nc.scalar.copy(
+                out=w_grouped[:, c, v_cols, :].rearrange("p (a i) t -> p a t i", i=4),
+                in_=four_rows[:, :, v_cols].rearrange("p t (a i) -> p a t i", i=4),
             )
         for c in range(PASSES):
             nc.vector.quantize_mx(
@@ -99,112 +253,25 @@ def tile_gemmaattention_pa_t_kernel(
                 in_=w_grouped[:, c].rearrange("p n t -> p (n t)"),
             )
 
-        hid_words = hid_sb[:].bitcast(F32)
+        def exists(i):
+            return 0 <= i < TILES
 
-        def prepare(g):
-            first = g * GROUP
-            hid_grouped = prep.tile([P, GROUP, HID], BF16, align_bytes=64)
-            grouped_words = hid_grouped[:].bitcast(F32)
-            for i in range(GROUP):
-                turned = psum_turn.tile([P, 2 * PASSES, P], F32)
-                for b in range(2 * PASSES):
-                    nc.tensor.transpose(
-                        turned[:, b, :], hid_words[:, first + i, b * P : (b + 1) * P], ident[:]
-                    )
-                nc.scalar.copy(
-                    out=grouped_words[:, i, :].rearrange("p (c s u) -> p c s u", c=PASSES, u=2),
-                    in_=turned[:].rearrange("p (c u) s -> p c s u", u=2),
-                )
-            hid_codes = prep.tile([P, GROUP * PASSES * P], U32, align_bytes=64)
-            hid_scales = prep.tile([P, GROUP * PASSES * P], U8, align_bytes=64)
-            nc.vector.quantize_mx(
-                out=hid_codes[:].bitcast(FP8X4),
-                scales=hid_scales[:],
-                in_=hid_grouped[:].rearrange("p g k -> p (g k)"),
-            )
-
-            table = prep.tile([P, GROUP, 2, 2, D], F32)
-            tiles = slice(first, first + GROUP)
-            gain_all = gain_ps[:].unsqueeze(1)
-            nc.vector.tensor_tensor(
-                out=table[:, :, :, 0, :],
-                in0=gain_all.to_broadcast([P, GROUP, 2, D]),
-                in1=cos_sb[:, tiles, :].unsqueeze(2).to_broadcast([P, GROUP, 2, D]),
-                op=ALU.mult,
-            )
-            for here, there in ((slice(0, HALF), slice(HALF, D)), (slice(HALF, D), slice(0, HALF))):
-                nc.vector.tensor_tensor(
-                    out=table[:, :, :, 1, here],
-                    in0=gain_all[:, :, :, here].to_broadcast([P, GROUP, 2, HALF]),
-                    in1=sin_sb[:, tiles, there].unsqueeze(2).to_broadcast([P, GROUP, 2, HALF]),
-                    op=ALU.mult,
-                )
-            return hid_codes, hid_scales, table
-
-        def project_norm_rotate(i, hid_codes, hid_scales, table, result):
-            q_ps = psum_acc.tile([P, BANK], F32)
-            kv_ps = psum_acc.tile([P, BANK], F32)
-            for c in range(PASSES):
-                rows = slice((i * PASSES + c) * P, (i * PASSES + c + 1) * P)
-                for bank, cols in ((q_ps, slice(0, BANK)), (kv_ps, slice(BANK, 2 * BANK))):
-                    nc.tensor.matmul_mx(
-                        out=bank[:],
-                        lhsT=hid_codes[:, rows].bitcast(FP8X4),
-                        lhsT_scale=hid_scales[:, rows],
-                        rhs=w_codes[:, c, cols].bitcast(FP8X4),
-                        rhs_scale=w_scales[:, c, cols],
-                        start=(c == 0),
-                        stop=(c == PASSES - 1),
-                    )
-            heads = [q_ps[:, h * D : (h + 1) * D] for h in range(Q_HEADS)]
-            heads += [kv_ps[:, h * D : (h + 1) * D] for h in range(K_HEADS)]
-
-            squares = work.tile([P, ROPE_HEADS, D], BF16)
-            sum_sq = work.tile([P, ROPE_HEADS], F32)
-            for h in range(ROPE_HEADS):
-                nc.scalar.activation(
-                    out=squares[:, h, :], in_=heads[h], func=ACT.Square, accum_out=sum_sq[:, h : h + 1]
-                )
-            nc.scalar.copy(out=result[:, ROPE_HEADS * D : N_OUT], in_=kv_ps[:, K_HEADS * D : BANK])
-            inv_rms = work.tile([P, ROPE_HEADS], F32)
-            nc.scalar.activation(
-                out=inv_rms[:], in_=sum_sq[:], func=ACT.Abs_reciprocal_sqrt, scale=1.0 / D, bias=EPS
-            )
-
-            products = work.tile([P, ROPE_HEADS, 2, D], F32)
-            for h in range(ROPE_HEADS):
-                nc.vector.scalar_tensor_tensor(
-                    out=products[:, h],
-                    in0=heads[h].unsqueeze(1).to_broadcast([P, 2, D]),
-                    scalar=inv_rms[:, h : h + 1],
-                    in1=table[:, i, 0 if h < Q_HEADS else 1],
-                    op0=ALU.mult,
-                    op1=ALU.mult,
-                )
-            rotated = result[:, 0 : ROPE_HEADS * D].rearrange("p (h d) -> p h d", d=D)
-            nc.gpsimd.tensor_tensor(
-                out=rotated[:, :, 0:HALF],
-                in0=products[:, :, 0, 0:HALF],
-                in1=products[:, :, 1, HALF:D],
-                op=ALU.subtract,
-            )
-            nc.gpsimd.tensor_tensor(
-                out=rotated[:, :, HALF:D],
-                in0=products[:, :, 0, HALF:D],
-                in1=products[:, :, 1, 0:HALF],
-                op=ALU.add,
-            )
-
-        ready = prepare(0)
-        for g in range(GROUPS):
-            current = ready
-            if g + 1 < GROUPS:
-                ready = prepare(g + 1)
-            for half in range(GROUP // STORE):
-                results = work.tile([P, STORE, N_OUT], F32)
-                for j in range(STORE):
-                    project_norm_rotate(half * STORE + j, current[0], current[1], current[2], results[:, j, :])
-                tiles = slice(g * GROUP + half * STORE, g * GROUP + (half + 1) * STORE)
-                nc.sync.dma_start(out=q_rows[:, tiles, :], in_=results[:, :, 0 : Q_HEADS * D])
-                nc.sync.dma_start(out=k_rows[:, tiles, :], in_=results[:, :, Q_HEADS * D : ROPE_HEADS * D])
-                nc.sync.dma_start(out=v_rows[:, tiles, :], in_=results[:, :, ROPE_HEADS * D : N_OUT])
+        for step in range(-LEAD_TURN, TILES + LAG_STORE):
+            if exists(step - LAG_STORE):
+                store(step - LAG_STORE)
+            if exists(step - LAG_ADD):
+                add_halves(step - LAG_ADD)
+            if exists(step):
+                multiply(step)
+            if exists(step + LEAD_NORM):
+                norm(step + LEAD_NORM)
+            if exists(step + LEAD_PROJECT):
+                project(step + LEAD_PROJECT)
+            if exists(step + LEAD_QUANTISE):
+                quantise_hidden(step + LEAD_QUANTISE)
+            if HEAD_TABLES <= step + LEAD_TABLE < TILES:
+                make_table(step + LEAD_TABLE)
+            if exists(step + LEAD_GROUP):
+                group_hidden(step + LEAD_GROUP)
+            if exists(step + LEAD_TURN):
+                turn_hidden(step + LEAD_TURN)

@@ -30,15 +30,15 @@ WORD_BLOCKS = HID // 2 // P
 TILES = SEQ // P
 PAIR = 2
 
-LEAD_TURN = 5
-LEAD_GROUP = 4
+LEAD_TURN = 6
+LEAD_GROUP = 5
 LEAD_QUANTISE = 3
 LEAD_PROJECT = 2
 LEAD_NORM = 1
 LAG_ADD = 1
 LAG_STORE = 2
 LEAD_TABLE = 7
-HEAD_TABLES = 4
+HEAD_PAIRS = 2
 EARLY_ANGLES = 8
 
 FLOPS = 2 * SEQ * HID * N_OUT
@@ -60,8 +60,9 @@ def tile_gemmaattention_pa_t_kernel(
     with ExitStack() as ctx:
         ctx.enter_context(tc.manual_schedule())
         keep = ctx.enter_context(tc.tile_pool(name="keep", bufs=1))
+        ahead = ctx.enter_context(tc.tile_pool(name="ahead", bufs=2))
         stage = ctx.enter_context(tc.tile_pool(name="stage", bufs=3))
-        tables = ctx.enter_context(tc.tile_pool(name="tables", bufs=LEAD_TABLE + 1))
+        tables = ctx.enter_context(tc.tile_pool(name="tables", bufs=LEAD_TABLE // PAIR + 2))
         leave = ctx.enter_context(tc.tile_pool(name="leave", bufs=4))
         psum_gain = ctx.enter_context(tc.psum_pool(name="psum_gain", bufs=1))
         psum_turn = ctx.enter_context(tc.psum_pool(name="psum_turn", bufs=2))
@@ -82,13 +83,15 @@ def tile_gemmaattention_pa_t_kernel(
             for t in range(first, last, PAIR):
                 nc.sync.dma_start(out=hid_sb[:, t : t + PAIR, :], in_=hid_rows[:, t : t + PAIR, :])
 
-        nc.sync.dma_start(out=cos_sb[:, 0:EARLY_ANGLES, :], in_=cos_rows[:, 0:EARLY_ANGLES, :])
-        nc.sync.dma_start(out=sin_sb[:, 0:EARLY_ANGLES, :], in_=sin_rows[:, 0:EARLY_ANGLES, :])
+        def load_angles(first, last):
+            nc.sync.dma_start(out=sin_sb[:, first:last, :], in_=sin_rows[:, first:last, :])
+            nc.sync.dma_start(out=cos_sb[:, first:last, :], in_=cos_rows[:, first:last, :])
+
+        load_angles(0, EARLY_ANGLES)
         for c in range(PASSES):
             nc.sync.dma_start(out=w_raw[:, c], in_=w_rows[:, c])
         load_hidden(0, EARLY_ANGLES)
-        nc.sync.dma_start(out=cos_sb[:, EARLY_ANGLES:TILES, :], in_=cos_rows[:, EARLY_ANGLES:TILES, :])
-        nc.sync.dma_start(out=sin_sb[:, EARLY_ANGLES:TILES, :], in_=sin_rows[:, EARLY_ANGLES:TILES, :])
+        load_angles(EARLY_ANGLES, TILES)
         load_hidden(EARLY_ANGLES, TILES)
 
         warm = keep.tile([P, 1], F32)
@@ -111,29 +114,30 @@ def tile_gemmaattention_pa_t_kernel(
         w_scales = keep.tile([P, PASSES, N_OUT], U8, align_bytes=64)
 
         table = {}
-        turned = {}
         grouped = {}
         hid_codes = {}
         hid_scales = {}
+        products = {}
+        results = {}
+        turned = {}
         q_ps = {}
         kv_ps = {}
         inv_rms = {}
-        products = {}
-        results = {}
 
-        def make_table(i):
-            table[i] = tables.tile([P, 2, 2, D], F32, name="table")
+        def make_table(pair):
+            table[pair] = tables.tile([P, PAIR, 2, 2, D], F32, name="table")
+            tiles = slice(pair * PAIR, (pair + 1) * PAIR)
             nc.vector.tensor_tensor(
-                out=table[i][:, :, 0, :],
-                in0=gain_ps[:],
-                in1=cos_sb[:, i, :].unsqueeze(1).to_broadcast([P, 2, D]),
+                out=table[pair][:, :, :, 0, :],
+                in0=gain_ps[:].unsqueeze(1).to_broadcast([P, PAIR, 2, D]),
+                in1=cos_sb[:, tiles, :].unsqueeze(2).to_broadcast([P, PAIR, 2, D]),
                 op=ALU.mult,
             )
             for here, there in ((slice(0, HALF), slice(HALF, D)), (slice(HALF, D), slice(0, HALF))):
                 nc.vector.tensor_tensor(
-                    out=table[i][:, :, 1, here],
-                    in0=gain_ps[:, :, here],
-                    in1=sin_sb[:, i, there].unsqueeze(1).to_broadcast([P, 2, HALF]),
+                    out=table[pair][:, :, :, 1, here],
+                    in0=gain_ps[:, :, here].unsqueeze(1).to_broadcast([P, PAIR, 2, HALF]),
+                    in1=sin_sb[:, tiles, there].unsqueeze(2).to_broadcast([P, PAIR, 2, HALF]),
                     op=ALU.mult,
                 )
 
@@ -143,17 +147,20 @@ def tile_gemmaattention_pa_t_kernel(
                 nc.tensor.transpose(turned[i][:, b, :], hid_words[:, i, b * P : (b + 1) * P], ident[:])
 
         def group_hidden(i):
-            grouped[i] = stage.tile([P, HID], BF16, name="grouped", align_bytes=64)
+            if i % PAIR == 0:
+                grouped[i // PAIR] = ahead.tile([P, PAIR, HID], BF16, name="grouped", align_bytes=64)
             nc.scalar.copy(
-                out=grouped[i][:].bitcast(F32).rearrange("p (c s u) -> p c s u", c=PASSES, u=2),
+                out=grouped[i // PAIR][:].bitcast(F32)[:, i % PAIR, :].rearrange("p (c s u) -> p c s u", c=PASSES, u=2),
                 in_=turned[i][:].rearrange("p (c u) s -> p c s u", u=2),
             )
 
-        def quantise_hidden(i):
-            hid_codes[i] = stage.tile([P, PASSES * P], U32, name="hid_codes", align_bytes=64)
-            hid_scales[i] = stage.tile([P, PASSES * P], U8, name="hid_scales", align_bytes=64)
+        def quantise_hidden(pair):
+            hid_codes[pair] = ahead.tile([P, PAIR * PASSES * P], U32, name="hid_codes", align_bytes=64)
+            hid_scales[pair] = ahead.tile([P, PAIR * PASSES * P], U8, name="hid_scales", align_bytes=64)
             nc.vector.quantize_mx(
-                out=hid_codes[i][:].bitcast(FP8X4), scales=hid_scales[i][:], in_=grouped[i][:]
+                out=hid_codes[pair][:].bitcast(FP8X4),
+                scales=hid_scales[pair][:],
+                in_=grouped[pair][:].rearrange("p t k -> p (t k)"),
             )
 
         def project(i):
@@ -161,11 +168,11 @@ def tile_gemmaattention_pa_t_kernel(
             kv_ps[i] = psum_kv.tile([P, BANK], F32, name="kv_ps")
             for bank, cols in ((q_ps[i], slice(0, BANK)), (kv_ps[i], slice(BANK, 2 * BANK))):
                 for c in range(PASSES):
-                    rows = slice(c * P, (c + 1) * P)
+                    rows = slice((i % PAIR * PASSES + c) * P, (i % PAIR * PASSES + c + 1) * P)
                     nc.tensor.matmul_mx(
                         out=bank[:],
-                        lhsT=hid_codes[i][:, rows].bitcast(FP8X4),
-                        lhsT_scale=hid_scales[i][:, rows],
+                        lhsT=hid_codes[i // PAIR][:, rows].bitcast(FP8X4),
+                        lhsT_scale=hid_scales[i // PAIR][:, rows],
                         rhs=w_codes[:, c, cols].bitcast(FP8X4),
                         rhs_scale=w_scales[:, c, cols],
                         start=(c == 0),
@@ -196,43 +203,45 @@ def tile_gemmaattention_pa_t_kernel(
             )
 
         def multiply(i):
-            products[i] = stage.tile([P, ROPE_HEADS, 2, D], F32, name="products")
+            if i % PAIR == 0:
+                products[i // PAIR] = stage.tile([P, PAIR, ROPE_HEADS, 2, D], F32, name="products")
             for h in list(range(Q_HEADS, ROPE_HEADS)) + list(range(Q_HEADS)):
                 nc.vector.scalar_tensor_tensor(
-                    out=products[i][:, h],
+                    out=products[i // PAIR][:, i % PAIR, h],
                     in0=head_of(i, h).unsqueeze(1).to_broadcast([P, 2, D]),
                     scalar=inv_rms[i][:, h : h + 1],
-                    in1=table[i][:, 0 if h < Q_HEADS else 1],
+                    in1=table[i // PAIR][:, i % PAIR, 0 if h < Q_HEADS else 1],
                     op0=ALU.mult,
                     op1=ALU.mult,
                 )
 
-        def add_halves(i):
-            rotated = result_of(i)[:, 0:ROPE_COLS].rearrange("p (h d) -> p h d", d=D)
-            nc.gpsimd.tensor_tensor(
-                out=rotated[:, :, 0:HALF],
-                in0=products[i][:, :, 0, 0:HALF],
-                in1=products[i][:, :, 1, HALF:D],
+        def add_halves(pair):
+            engine = nc.vector if pair == TILES // PAIR - 1 else nc.gpsimd
+            rotated = results[pair][:, :, 0:ROPE_COLS].rearrange("p t (h d) -> p t h d", d=D)
+            engine.tensor_tensor(
+                out=rotated[:, :, :, 0:HALF],
+                in0=products[pair][:, :, :, 0, 0:HALF],
+                in1=products[pair][:, :, :, 1, HALF:D],
                 op=ALU.subtract,
             )
-            nc.gpsimd.tensor_tensor(
-                out=rotated[:, :, HALF:D],
-                in0=products[i][:, :, 0, HALF:D],
-                in1=products[i][:, :, 1, 0:HALF],
+            engine.tensor_tensor(
+                out=rotated[:, :, :, HALF:D],
+                in0=products[pair][:, :, :, 0, HALF:D],
+                in1=products[pair][:, :, :, 1, 0:HALF],
                 op=ALU.add,
             )
 
-        def store(i):
-            if i % PAIR != PAIR - 1:
-                return
-            pair = results[i // PAIR]
-            tiles = slice(i - PAIR + 1, i + 1)
-            nc.sync.dma_start(out=q_rows[:, tiles, :], in_=pair[:, :, 0 : Q_HEADS * D])
-            nc.sync.dma_start(out=k_rows[:, tiles, :], in_=pair[:, :, Q_HEADS * D : ROPE_COLS])
-            nc.sync.dma_start(out=v_rows[:, tiles, :], in_=pair[:, :, ROPE_COLS:N_OUT])
+        def store_v(pair):
+            tiles = slice(pair * PAIR, (pair + 1) * PAIR)
+            nc.sync.dma_start(out=v_rows[:, tiles, :], in_=results[pair][:, :, ROPE_COLS:N_OUT])
 
-        for i in range(HEAD_TABLES):
-            make_table(i)
+        def store_q_k(pair):
+            tiles = slice(pair * PAIR, (pair + 1) * PAIR)
+            nc.sync.dma_start(out=q_rows[:, tiles, :], in_=results[pair][:, :, 0 : Q_HEADS * D])
+            nc.sync.dma_start(out=k_rows[:, tiles, :], in_=results[pair][:, :, Q_HEADS * D : ROPE_COLS])
+
+        for pair in range(HEAD_PAIRS):
+            make_table(pair)
 
         rope_cols = slice(0, ROPE_COLS)
         v_cols = slice(ROPE_COLS, N_OUT)
@@ -256,21 +265,29 @@ def tile_gemmaattention_pa_t_kernel(
         def exists(i):
             return 0 <= i < TILES
 
+        def first_of_pair(i):
+            return exists(i) and i % PAIR == 0
+
+        def last_of_pair(i):
+            return exists(i) and i % PAIR == PAIR - 1
+
         for step in range(-LEAD_TURN, TILES + LAG_STORE):
-            if exists(step - LAG_STORE):
-                store(step - LAG_STORE)
-            if exists(step - LAG_ADD):
-                add_halves(step - LAG_ADD)
+            if last_of_pair(step - LAG_STORE):
+                store_q_k((step - LAG_STORE) // PAIR)
+            if last_of_pair(step - LAG_ADD):
+                add_halves((step - LAG_ADD) // PAIR)
+            if last_of_pair(step):
+                store_v(step // PAIR)
             if exists(step):
                 multiply(step)
             if exists(step + LEAD_NORM):
                 norm(step + LEAD_NORM)
             if exists(step + LEAD_PROJECT):
                 project(step + LEAD_PROJECT)
-            if exists(step + LEAD_QUANTISE):
-                quantise_hidden(step + LEAD_QUANTISE)
-            if HEAD_TABLES <= step + LEAD_TABLE < TILES:
-                make_table(step + LEAD_TABLE)
+            if first_of_pair(step + LEAD_QUANTISE):
+                quantise_hidden((step + LEAD_QUANTISE) // PAIR)
+            if first_of_pair(step + LEAD_TABLE) and (step + LEAD_TABLE) // PAIR >= HEAD_PAIRS:
+                make_table((step + LEAD_TABLE) // PAIR)
             if exists(step + LEAD_GROUP):
                 group_hidden(step + LEAD_GROUP)
             if exists(step + LEAD_TURN):

from contextlib import ExitStack

import concourse.mybir as mybir
from concourse.masks import make_identity

F32 = mybir.dt.float32
BF16 = mybir.dt.bfloat16
U32 = mybir.dt.uint32
U8 = mybir.dt.uint8
FP8X4 = mybir.dt.float8_e4m3fn_x4
ALU = mybir.AluOpType
ACT = mybir.ActivationFunctionType

P = 128
SEQ = 4096
HID = 1024
D = 128
HALF = D // 2
Q_HEADS = 4
K_HEADS = 2
ROPE_HEADS = Q_HEADS + K_HEADS
ROPE_COLS = ROPE_HEADS * D
N_OUT = 1024
BANK = 512
EPS = 1e-6

K_PASS = 512
PASSES = HID // K_PASS
WORD_BLOCKS = HID // 2 // P
TILES = SEQ // P
PAIR = 2

LEAD_TURN = 6
LEAD_GROUP = 5
LEAD_QUANTISE = 3
LEAD_PROJECT = 2
LEAD_NORM = 1
LAG_ADD = 1
LAG_STORE = 2
LEAD_TABLE = 7
HEAD_PAIRS = 2
EARLY_ANGLES = 8

FLOPS = 2 * SEQ * HID * N_OUT


def tile_gemmaattention_pa_t_kernel(
    tc, hidden_states, w_qkv, q_norm_w, k_norm_w, cos, sin, out_0, out_1, out_2
):
    nc = tc.nc

    hid_rows = hidden_states.rearrange("(p t) k -> p t k", t=TILES)
    cos_rows = cos.rearrange("(p t) d -> p t d", t=TILES)
    sin_rows = sin.rearrange("(p t) d -> p t d", t=TILES)
    q_rows = out_0.rearrange("(p t) h d -> p t (h d)", t=TILES)
    k_rows = out_1.rearrange("(p t) h d -> p t (h d)", t=TILES)
    v_rows = out_2.rearrange("(p t) h d -> p t (h d)", t=TILES)
    w_rows = w_qkv.rearrange("(c u p e) n -> p c u (e n)", c=PASSES, u=2, p=P, e=2)

    with ExitStack() as ctx:
        ctx.enter_context(tc.manual_schedule())
        keep = ctx.enter_context(tc.tile_pool(name="keep", bufs=1))
        ahead = ctx.enter_context(tc.tile_pool(name="ahead", bufs=2))
        stage = ctx.enter_context(tc.tile_pool(name="stage", bufs=3))
        tables = ctx.enter_context(tc.tile_pool(name="tables", bufs=LEAD_TABLE // PAIR + 2))
        leave = ctx.enter_context(tc.tile_pool(name="leave", bufs=4))
        psum_gain = ctx.enter_context(tc.psum_pool(name="psum_gain", bufs=1))
        psum_turn = ctx.enter_context(tc.psum_pool(name="psum_turn", bufs=2))
        psum_q = ctx.enter_context(tc.psum_pool(name="psum_q", bufs=3))
        psum_kv = ctx.enter_context(tc.psum_pool(name="psum_kv", bufs=2))

        hid_sb = keep.tile([P, TILES, HID], BF16)
        w_raw = keep.tile([P, PASSES, 2, 2 * N_OUT], BF16)
        cos_sb = keep.tile([P, TILES, D], BF16)
        sin_sb = keep.tile([P, TILES, D], BF16)
        gain_rows = keep.tile([P, 2 * D], BF16)
        nc.vector.memset(gain_rows[:], 0.0)
        nc.vector.memset(gain_rows[32:33, :], 1.0)
        nc.sync.dma_start(out=gain_rows[0:1, 0:D], in_=q_norm_w.rearrange("(o d) -> o d", o=1))
        nc.sync.dma_start(out=gain_rows[0:1, D : 2 * D], in_=k_norm_w.rearrange("(o d) -> o d", o=1))

        def load_hidden(first, last):
            for t in range(first, last, PAIR):
                nc.sync.dma_start(out=hid_sb[:, t : t + PAIR, :], in_=hid_rows[:, t : t + PAIR, :])

        def load_angles(first, last):
            nc.sync.dma_start(out=sin_sb[:, first:last, :], in_=sin_rows[:, first:last, :])
            nc.sync.dma_start(out=cos_sb[:, first:last, :], in_=cos_rows[:, first:last, :])

        load_angles(0, EARLY_ANGLES)
        for c in range(PASSES):
            nc.sync.dma_start(out=w_raw[:, c], in_=w_rows[:, c])
        load_hidden(0, EARLY_ANGLES)
        load_angles(EARLY_ANGLES, TILES)
        load_hidden(EARLY_ANGLES, TILES)

        warm = keep.tile([P, 1], F32)
        nc.vector.memset(warm[:], 1.0)
        nc.scalar.activation(out=warm[:], in_=warm[:], func=ACT.Abs_reciprocal_sqrt)

        ident = keep.tile([P, P], F32)
        make_identity(nc, ident[:])

        ones = keep.tile([P, P], BF16)
        nc.vector.memset(ones[:], 1.0)
        gain_ps = psum_gain.tile([P, 2, D], F32)
        nc.tensor.matmul(
            gain_ps[:].rearrange("p c d -> p (c d)"), lhsT=ones[:], rhs=gain_rows[:], start=True, stop=True
        )

        hid_words = hid_sb[:].bitcast(F32)
        w_grouped = keep.tile([P, PASSES, N_OUT, 4], BF16, align_bytes=64)
        w_codes = keep.tile([P, PASSES, N_OUT], U32, align_bytes=64)
        w_scales = keep.tile([P, PASSES, N_OUT], U8, align_bytes=64)

        table = {}
        grouped = {}
        hid_codes = {}
        hid_scales = {}
        products = {}
        results = {}
        turned = {}
        q_ps = {}
        kv_ps = {}
        inv_rms = {}

        def make_table(pair):
            table[pair] = tables.tile([P, PAIR, 2, 2, D], F32, name="table")
            tiles = slice(pair * PAIR, (pair + 1) * PAIR)
            nc.vector.tensor_tensor(
                out=table[pair][:, :, :, 0, :],
                in0=gain_ps[:].unsqueeze(1).to_broadcast([P, PAIR, 2, D]),
                in1=cos_sb[:, tiles, :].unsqueeze(2).to_broadcast([P, PAIR, 2, D]),
                op=ALU.mult,
            )
            for here, there in ((slice(0, HALF), slice(HALF, D)), (slice(HALF, D), slice(0, HALF))):
                nc.vector.tensor_tensor(
                    out=table[pair][:, :, :, 1, here],
                    in0=gain_ps[:, :, here].unsqueeze(1).to_broadcast([P, PAIR, 2, HALF]),
                    in1=sin_sb[:, tiles, there].unsqueeze(2).to_broadcast([P, PAIR, 2, HALF]),
                    op=ALU.mult,
                )

        def turn_hidden(i):
            turned[i] = psum_turn.tile([P, WORD_BLOCKS, P], F32, name="turned")
            for b in range(WORD_BLOCKS):
                nc.tensor.transpose(turned[i][:, b, :], hid_words[:, i, b * P : (b + 1) * P], ident[:])

        def group_hidden(i):
            if i % PAIR == 0:
                grouped[i // PAIR] = ahead.tile([P, PAIR, HID], BF16, name="grouped", align_bytes=64)
            nc.scalar.copy(
                out=grouped[i // PAIR][:].bitcast(F32)[:, i % PAIR, :].rearrange("p (c s u) -> p c s u", c=PASSES, u=2),
                in_=turned[i][:].rearrange("p (c u) s -> p c s u", u=2),
            )

        def quantise_hidden(pair):
            hid_codes[pair] = ahead.tile([P, PAIR * PASSES * P], U32, name="hid_codes", align_bytes=64)
            hid_scales[pair] = ahead.tile([P, PAIR * PASSES * P], U8, name="hid_scales", align_bytes=64)
            nc.vector.quantize_mx(
                out=hid_codes[pair][:].bitcast(FP8X4),
                scales=hid_scales[pair][:],
                in_=grouped[pair][:].rearrange("p t k -> p (t k)"),
            )

        def project(i):
            q_ps[i] = psum_q.tile([P, BANK], F32, name="q_ps")
            kv_ps[i] = psum_kv.tile([P, BANK], F32, name="kv_ps")
            for bank, cols in ((q_ps[i], slice(0, BANK)), (kv_ps[i], slice(BANK, 2 * BANK))):
                for c in range(PASSES):
                    rows = slice((i % PAIR * PASSES + c) * P, (i % PAIR * PASSES + c + 1) * P)
                    nc.tensor.matmul_mx(
                        out=bank[:],
                        lhsT=hid_codes[i // PAIR][:, rows].bitcast(FP8X4),
                        lhsT_scale=hid_scales[i // PAIR][:, rows],
                        rhs=w_codes[:, c, cols].bitcast(FP8X4),
                        rhs_scale=w_scales[:, c, cols],
                        start=(c == 0),
                        stop=(c == PASSES - 1),
                    )

        def head_of(i, h):
            if h < Q_HEADS:
                return q_ps[i][:, h * D : (h + 1) * D]
            return kv_ps[i][:, (h - Q_HEADS) * D : (h - Q_HEADS + 1) * D]

        def result_of(i):
            return results[i // PAIR][:, i % PAIR, :]

        def norm(i):
            if i % PAIR == 0:
                results[i // PAIR] = leave.tile([P, PAIR, N_OUT], F32, name="results")
            squares = stage.tile([P, ROPE_HEADS, D], BF16, name="squares")
            sum_sq = stage.tile([P, ROPE_HEADS], F32, name="sum_sq")
            for h in range(ROPE_HEADS):
                nc.scalar.activation(
                    out=squares[:, h, :], in_=head_of(i, h), func=ACT.Square, accum_out=sum_sq[:, h : h + 1]
                )
            nc.scalar.copy(out=result_of(i)[:, ROPE_COLS:N_OUT], in_=kv_ps[i][:, K_HEADS * D : BANK])
            inv_rms[i] = stage.tile([P, ROPE_HEADS], F32, name="inv_rms")
            nc.scalar.activation(
                out=inv_rms[i][:], in_=sum_sq[:], func=ACT.Abs_reciprocal_sqrt, scale=1.0 / D, bias=EPS
            )

        def multiply(i):
            if i % PAIR == 0:
                products[i // PAIR] = stage.tile([P, PAIR, ROPE_HEADS, 2, D], F32, name="products")
            for h in list(range(Q_HEADS, ROPE_HEADS)) + list(range(Q_HEADS)):
                nc.vector.scalar_tensor_tensor(
                    out=products[i // PAIR][:, i % PAIR, h],
                    in0=head_of(i, h).unsqueeze(1).to_broadcast([P, 2, D]),
                    scalar=inv_rms[i][:, h : h + 1],
                    in1=table[i // PAIR][:, i % PAIR, 0 if h < Q_HEADS else 1],
                    op0=ALU.mult,
                    op1=ALU.mult,
                )

        def add_halves(pair):
            engine = nc.vector if pair == TILES // PAIR - 1 else nc.gpsimd
            rotated = results[pair][:, :, 0:ROPE_COLS].rearrange("p t (h d) -> p t h d", d=D)
            engine.tensor_tensor(
                out=rotated[:, :, :, 0:HALF],
                in0=products[pair][:, :, :, 0, 0:HALF],
                in1=products[pair][:, :, :, 1, HALF:D],
                op=ALU.subtract,
            )
            engine.tensor_tensor(
                out=rotated[:, :, :, HALF:D],
                in0=products[pair][:, :, :, 0, HALF:D],
                in1=products[pair][:, :, :, 1, 0:HALF],
                op=ALU.add,
            )

        def store_v(pair):
            tiles = slice(pair * PAIR, (pair + 1) * PAIR)
            nc.sync.dma_start(out=v_rows[:, tiles, :], in_=results[pair][:, :, ROPE_COLS:N_OUT])

        def store_q_k(pair):
            tiles = slice(pair * PAIR, (pair + 1) * PAIR)
            nc.sync.dma_start(out=q_rows[:, tiles, :], in_=results[pair][:, :, 0 : Q_HEADS * D])
            nc.sync.dma_start(out=k_rows[:, tiles, :], in_=results[pair][:, :, Q_HEADS * D : ROPE_COLS])

        for pair in range(HEAD_PAIRS):
            make_table(pair)

        rope_cols = slice(0, ROPE_COLS)
        v_cols = slice(ROPE_COLS, N_OUT)
        for c in range(PASSES):
            four_rows = w_raw[:, c].rearrange("p u (e n) -> p (u e) n", e=2)
            nc.vector.tensor_copy(
                out=w_grouped[:, c, rope_cols, :].rearrange("p (a i) t -> p a t i", i=4),
                in_=four_rows[:, :, rope_cols].rearrange("p t (a i) -> p a t i", i=4),
            )
            nc.scalar.copy(
                out=w_grouped[:, c, v_cols, :].rearrange("p (a i) t -> p a t i", i=4),
                in_=four_rows[:, :, v_cols].rearrange("p t (a i) -> p a t i", i=4),
            )
        for c in range(PASSES):
            nc.vector.quantize_mx(
                out=w_codes[:, c, :].bitcast(FP8X4),
                scales=w_scales[:, c, :],
                in_=w_grouped[:, c].rearrange("p n t -> p (n t)"),
            )

        def exists(i):
            return 0 <= i < TILES

        def first_of_pair(i):
            return exists(i) and i % PAIR == 0

        def last_of_pair(i):
            return exists(i) and i % PAIR == PAIR - 1

        for step in range(-LEAD_TURN, TILES + LAG_STORE):
            if last_of_pair(step - LAG_STORE):
                store_q_k((step - LAG_STORE) // PAIR)
            if last_of_pair(step - LAG_ADD):
                add_halves((step - LAG_ADD) // PAIR)
            if last_of_pair(step):
                store_v(step // PAIR)
            if exists(step):
                multiply(step)
            if exists(step + LEAD_NORM):
                norm(step + LEAD_NORM)
            if exists(step + LEAD_PROJECT):
                project(step + LEAD_PROJECT)
            if first_of_pair(step + LEAD_QUANTISE):
                quantise_hidden((step + LEAD_QUANTISE) // PAIR)
            if first_of_pair(step + LEAD_TABLE) and (step + LEAD_TABLE) // PAIR >= HEAD_PAIRS:
                make_table((step + LEAD_TABLE) // PAIR)
            if exists(step + LEAD_GROUP):
                group_hidden(step + LEAD_GROUP)
            if exists(step + LEAD_TURN):
                turn_hidden(step + LEAD_TURN)
